import numpy as np
import ml_dtypes


def mxq(x, axis, fmt="e4m3"):
    dtype, down = {"e4m3": (ml_dtypes.float8_e4m3fn, 7), "e5m2": (ml_dtypes.float8_e5m2, 14)}[fmt]
    v = np.moveaxis(np.asarray(x, np.float32).astype(ml_dtypes.bfloat16).astype(np.float64), axis, -1)
    blocks = v.reshape(v.shape[:-1] + (-1, 32))
    amax = np.abs(blocks).max(-1, keepdims=True)
    byte = np.maximum(np.where(amax > 0, np.frexp(amax)[1] - 1 + 127, 0) - down, 1)
    scale = np.exp2(byte - 127.0)
    codes = (blocks / scale).astype(np.float32).astype(dtype).astype(np.float64)
    return np.moveaxis((codes * scale).reshape(v.shape), -1, axis)


WIDE = False


def mx_kscale(k):
    if not WIDE:
        return np.ones(k)
    levels = np.array([10, -10, 5, -5, 0])
    a = np.random.permutation(np.resize(levels, k // 512 * 4)).reshape(k // 512, 4)
    idx = np.arange(k)
    return np.exp2(a[idx // 512, idx % 128 // 32])


BF16 = ml_dtypes.bfloat16


def bf(x):
    return np.asarray(x, np.float32).astype(BF16)


def f64(x):
    return np.asarray(x).astype(np.float64)


B, H, L, E, QD = 64, 1, 128, 1024, 128
EPS = 1e-5


def build_decay_mask(num_heads, max_len):
    r = f64(np.arange(max_len))
    dec = np.array([1.0 - 2.0 ** (-5 - h) for h in range(num_heads)])
    expo = r[None, :] - r[:, None]
    return np.where(r[:, None] >= r[None, :], dec[:, None, None] ** expo[None], 0.0)


def setup_inputs():
    s = mx_kscale(E)
    kv = (0.1 + 0.32 * np.random.standard_normal((B, H, L, QD))) * (0.1 + 0.32 * np.random.standard_normal((B, H, L, QD)))
    return {"x": bf(np.random.standard_normal((B, H, L, E)) * s),
            "Wq": bf(np.random.standard_normal((QD, E)) / np.sqrt(E) / s),
            "bq": bf(0.3 + 0.3 * np.random.standard_normal(QD)),
            "kv": bf(kv),
            "decay_mask": bf(build_decay_mask(H, L))}


def reference(x, Wq, bq, kv, decay_mask):
    b, h, l, e = x.shape
    Q = (mxq(f64(x), 3, "e4m3") @ mxq(f64(Wq), 1, "e4m3").T) + f64(bq)
    D = f64(decay_mask)[0, :l, :l]
    y = Q * (f64(kv) @ D.T)
    mean = y.mean(axis=(2, 3), keepdims=True)
    var = ((y - mean) ** 2).mean(axis=(2, 3), keepdims=True)
    y = (y - mean) / np.sqrt(var + EPS)
    return y.reshape(b, l, -1)

@@ -1,0 +1,250 @@
+from contextlib import ExitStack
+
+import concourse.mybir as mybir
+from concourse.masks import make_identity
+
+F32 = mybir.dt.float32
+BF16 = mybir.dt.bfloat16
+U32 = mybir.dt.uint32
+U8 = mybir.dt.uint8
+FP8X4 = mybir.dt.float8_e4m3fn_x4
+ALU = mybir.AluOpType
+ACT = mybir.ActivationFunctionType
+
+P = 128
+B, L, E, QD = 64, 128, 1024, 128
+EPS = 1e-5
+PACK = 4
+K_PASS = P * PACK
+PASSES = E // K_PASS
+HALVES = 2
+J = 4
+GROUP_TOKENS = P * J
+GROUPS = B * L // GROUP_TOKENS
+SAMPLE_PARTITIONS = L // J
+KV_CHUNK = 4
+
+FLOPS = 2 * B * L * QD * E + 2 * B * L * QD * L
+
+
+def tile_parallelretention_pb_t_kernel(tc, x, Wq, bq, kv, decay_mask, out):
+    nc = tc.nc
+    x_groups = x.rearrange("n h l e -> (n h l) e").rearrange("(g p j) e -> g p (j e)", p=P, j=J)
+    kv_chunks = kv.rearrange("n h l k -> (n h l) k").rearrange(
+        "(a g p j) k -> a p g (j k)", g=KV_CHUNK, p=P, j=J
+    )
+    out_groups = out.rearrange("n l q -> (n l) q").rearrange("(g p j) q -> g p (j q)", p=P, j=J)
+
+    with ExitStack() as ctx:
+        consts = ctx.enter_context(tc.tile_pool(name="consts", bufs=1))
+        resident = ctx.enter_context(tc.tile_pool(name="resident", bufs=1))
+        work = ctx.enter_context(tc.tile_pool(name="work", bufs=2))
+        psum = ctx.enter_context(tc.psum_pool(name="psum", bufs=1))
+
+        w_sb = consts.tile([P, E], BF16)
+        nc.scalar.dma_start(out=w_sb[:], in_=Wq)
+        d_sb = consts.tile([P, L], BF16)
+        nc.scalar.dma_start(out=d_sb[:], in_=decay_mask[0])
+        bias_rows = consts.tile([P, QD], BF16)
+        nc.scalar.dma_start(out=bias_rows[:], in_=bq.partition_broadcast(P))
+
+        x_tiles = []
+        kv_tiles = []
+        for g in range(GROUPS):
+            x_sb = resident.tile([P, J * E], BF16, name="x_sb", bufs=GROUPS)
+            nc.sync.dma_start(out=x_sb[:], in_=x_groups[g])
+            x_tiles.append(x_sb)
+            if g % KV_CHUNK == 0:
+                kv_sb = resident.tile([P, KV_CHUNK, J * L], BF16, name="kv_sb", bufs=GROUPS // KV_CHUNK)
+                nc.sync.dma_start(out=kv_sb[:], in_=kv_chunks[g // KV_CHUNK])
+                kv_tiles.append(kv_sb)
+
+        ident_f32 = consts.tile([P, P], F32)
+        make_identity(nc, ident_f32[:])
+        ident_bf = consts.tile([P, P], BF16)
+        make_identity(nc, ident_bf[:])
+        sample_mean = consts.tile([P, P], F32)
+        nc.vector.memset(sample_mean[:], 0.0)
+        for s in range(P // SAMPLE_PARTITIONS):
+            rows = slice(s * SAMPLE_PARTITIONS, (s + 1) * SAMPLE_PARTITIONS)
+            nc.vector.memset(sample_mean[rows, rows], 1.0 / (L * QD))
+        one = consts.tile([P, 1], F32)
+        nc.vector.memset(one[:], 1.0)
+        eps = consts.tile([P, 1], F32)
+        nc.vector.memset(eps[:], EPS)
+        warm = consts.tile([P, 1], F32)
+        nc.scalar.activation(out=warm[:], in_=one[:], func=ACT.Sqrt)
+
+        def transpose_words(rows_bf16, grouped_words, copy):
+            words = rows_bf16.bitcast(F32).rearrange("p (c u w) -> p c u w", c=PASSES, u=HALVES)
+            flipped = psum.tile([P, PASSES, HALVES, P], F32, tag="flipped", bufs=4)
+            for c in range(PASSES):
+                for u in range(HALVES):
+                    nc.tensor.transpose(flipped[:, c, u, :], words[:, c, u, :], ident_f32[:])
+            copy(out=grouped_words, in_=flipped[:].rearrange("p c u r -> p c r u"))
+
+        w_grouped = consts.tile([P, PASSES * QD * PACK], BF16, align_bytes=64)
+        transpose_words(
+            w_sb[:],
+            w_grouped[:].bitcast(F32).rearrange("p (c r u) -> p c r u", c=PASSES, u=HALVES),
+            nc.vector.tensor_copy,
+        )
+        w_codes = consts.tile([P, PASSES * QD], U32, align_bytes=64)
+        w_scales = consts.tile([P, PASSES * QD], U8, align_bytes=64)
+        nc.vector.quantize_mx(out=w_codes[:].bitcast(FP8X4), scales=w_scales[:], in_=w_grouped[:])
+
+        d_flipped = psum.tile([P, P], BF16, tag="flipped", bufs=4)
+        nc.tensor.transpose(d_flipped[:], d_sb[:], ident_bf[:])
+        d_t = consts.tile([P, QD], BF16)
+        nc.vector.tensor_copy(out=d_t[:], in_=d_flipped[:])
+
+        grouped_tiles = {}
+        code_tiles = {}
+        kv_t_tiles = {}
+        psum_tiles = {}
+        y_tiles = {}
+        stat_tiles = {}
+
+        def flip_x(g):
+            grouped = work.tile([P, J * PASSES * P * PACK], BF16, align_bytes=64)
+            grouped_words = grouped[:].bitcast(F32).rearrange(
+                "p (j c r u) -> p j c r u", j=J, c=PASSES, u=HALVES
+            )
+            for j in range(J):
+                transpose_words(x_tiles[g][:, j * E : (j + 1) * E], grouped_words[:, j], nc.scalar.copy)
+            grouped_tiles[g] = grouped
+
+        def flip_kv(g):
+            kv_flipped = psum.tile([P, J, P], BF16, tag="flipped", bufs=4)
+            for j in range(J):
+                nc.tensor.transpose(
+                    kv_flipped[:, j, :],
+                    kv_tiles[g // KV_CHUNK][:, g % KV_CHUNK, j * L : (j + 1) * L],
+                    ident_bf[:],
+                )
+            kv_t = work.tile([P, J, P], BF16, bufs=3)
+            nc.vector.tensor_copy(out=kv_t[:], in_=kv_flipped[:])
+            kv_t_tiles[g] = kv_t
+
+        def quantise(g):
+            codes = work.tile([P, J * PASSES * P], U32, align_bytes=64)
+            scales = work.tile([P, J * PASSES * P], U8, align_bytes=64)
+            nc.vector.quantize_mx(
+                out=codes[:].bitcast(FP8X4), scales=scales[:], in_=grouped_tiles[g][:]
+            )
+            code_tiles[g] = (codes, scales)
+
+        def multiply(g):
+            codes, scales = code_tiles[g]
+            q_ps = psum.tile([P, J, QD], F32)
+            for j in range(J):
+                for c in range(PASSES):
+                    cols = slice((j * PASSES + c) * P, (j * PASSES + c + 1) * P)
+                    w_cols = slice(c * QD, (c + 1) * QD)
+                    nc.tensor.matmul_mx(
+                        out=q_ps[:, j, :],
+                        lhsT=codes[:, cols].bitcast(FP8X4),
+                        lhsT_scale=scales[:, cols],
+                        rhs=w_codes[:, w_cols].bitcast(FP8X4),
+                        rhs_scale=w_scales[:, w_cols],
+                        start=(c == 0),
+                        stop=(c == PASSES - 1),
+                    )
+            g_ps = psum.tile([P, J, QD], F32)
+            for j in range(J):
+                nc.tensor.matmul(
+                    out=g_ps[:, j, :], lhsT=kv_t_tiles[g][:, j, :], rhs=d_t[:], start=True, stop=True
+                )
+            psum_tiles[g] = (q_ps, g_ps)
+
+        def product(g):
+            q_ps, g_ps = psum_tiles[g]
+            q_biased = work.tile([P, J, QD], F32)
+            nc.vector.tensor_tensor(
+                out=q_biased[:],
+                in0=q_ps[:],
+                in1=bias_rows[:].unsqueeze(1).to_broadcast([P, J, QD]),
+                op=ALU.add,
+            )
+            y = resident.tile([P, J * QD], F32, name="y", bufs=GROUPS)
+            y_sum = work.tile([P, 1], F32, bufs=6)
+            nc.vector.scalar_tensor_tensor(
+                out=y[:],
+                in0=q_biased[:].rearrange("p j q -> p (j q)"),
+                scalar=1.0,
+                in1=g_ps[:].rearrange("p j q -> p (j q)"),
+                op0=ALU.mult,
+                op1=ALU.mult,
+                accum_out=y_sum[:],
+            )
+            y_tiles[g] = y
+            stat_tiles[g] = {"y_sum": y_sum}
+
+        def mean(g):
+            mean_ps = psum.tile([P, 1], F32)
+            nc.tensor.matmul(
+                out=mean_ps[:], lhsT=sample_mean[:], rhs=stat_tiles[g]["y_sum"][:], start=True, stop=True
+            )
+            neg_mean = work.tile([P, 1], F32, bufs=6)
+            nc.vector.tensor_scalar(
+                out=neg_mean[:], in0=mean_ps[:], scalar1=-1.0, scalar2=None, op0=ALU.mult
+            )
+            stat_tiles[g]["neg_mean"] = neg_mean
+
+        def squares(g):
+            squared = work.tile([P, J * QD], BF16, bufs=2)
+            sq_sum = work.tile([P, 1], F32, bufs=6)
+            nc.scalar.activation(
+                out=squared[:],
+                in_=y_tiles[g][:],
+                func=ACT.Square,
+                bias=stat_tiles[g]["neg_mean"][:],
+                scale=1.0,
+                accum_out=sq_sum[:],
+            )
+            stat_tiles[g]["sq_sum"] = sq_sum
+
+        def variance(g):
+            var_ps = psum.tile([P, 1], F32)
+            nc.tensor.matmul(
+                out=var_ps[:], lhsT=sample_mean[:], rhs=stat_tiles[g]["sq_sum"][:], start=True, stop=True
+            )
+            stat_tiles[g]["var_ps"] = var_ps
+
+        def deviation(g):
+            std = work.tile([P, 1], F32, bufs=6)
+            nc.scalar.activation(
+                out=std[:], in_=stat_tiles[g]["var_ps"][:], func=ACT.Sqrt, bias=eps[:], scale=1.0
+            )
+            stat_tiles[g]["std"] = std
+
+        def finish(g):
+            rstd = work.tile([P, 1], F32, bufs=6)
+            nc.vector.reciprocal(out=rstd[:], in_=stat_tiles[g]["std"][:])
+            y = y_tiles[g]
+            nc.vector.tensor_scalar(
+                out=y[:],
+                in0=y[:],
+                scalar1=stat_tiles[g]["neg_mean"][:],
+                scalar2=rstd[:],
+                op0=ALU.add,
+                op1=ALU.mult,
+            )
+            nc.sync.dma_start(out=out_groups[g], in_=y[:])
+
+        def run(stage, g):
+            if 0 <= g < GROUPS:
+                stage(g)
+
+        with tc.manual_schedule():
+            for k in range(-1, GROUPS + 3):
+                run(flip_x, k + 1)
+                run(quantise, k)
+                run(mean, k - 1)
+                run(variance, k - 2)
+                run(squares, k - 1)
+                run(deviation, k - 2)
+                run(finish, k - 3)
+                run(flip_kv, k + 1)
+                run(multiply, k)
+                run(product, k)

@@ -100,30 +100,35 @@ def tile_parallelretention_pb_t_kernel(tc, x, Wq, bq, kv, decay_mask, out):
 
         grouped_tiles = {}
         code_tiles = {}
+        kv_flipped_tiles = {}
         kv_t_tiles = {}
         psum_tiles = {}
         y_tiles = {}
         stat_tiles = {}
 
-        def flip_x(g):
-            grouped = work.tile([P, J * PASSES * P * PACK], BF16, align_bytes=64)
-            grouped_words = grouped[:].bitcast(F32).rearrange(
+        def flip_x(g, rows):
+            if g not in grouped_tiles:
+                grouped = work.tile([P, J * PASSES * P * PACK], BF16, align_bytes=64)
+                grouped_tiles[g] = grouped
+            grouped_words = grouped_tiles[g][:].bitcast(F32).rearrange(
                 "p (j c r u) -> p j c r u", j=J, c=PASSES, u=HALVES
             )
-            for j in range(J):
+            for j in rows:
                 transpose_words(x_tiles[g][:, j * E : (j + 1) * E], grouped_words[:, j], nc.scalar.copy)
-            grouped_tiles[g] = grouped
 
         def flip_kv(g):
             kv_flipped = psum.tile([P, J, P], BF16, tag="flipped", bufs=4)
+            kv_flipped_tiles[g] = kv_flipped
             for j in range(J):
                 nc.tensor.transpose(
                     kv_flipped[:, j, :],
                     kv_tiles[g // KV_CHUNK][:, g % KV_CHUNK, j * L : (j + 1) * L],
                     ident_bf[:],
                 )
+
+        def copy_kv(g):
             kv_t = work.tile([P, J, P], BF16, bufs=3)
-            nc.vector.tensor_copy(out=kv_t[:], in_=kv_flipped[:])
+            nc.vector.tensor_copy(out=kv_t[:], in_=kv_flipped_tiles[g][:])
             kv_t_tiles[g] = kv_t
 
         def quantise(g):
@@ -185,9 +190,12 @@ def tile_parallelretention_pb_t_kernel(tc, x, Wq, bq, kv, decay_mask, out):
             nc.tensor.matmul(
                 out=mean_ps[:], lhsT=sample_mean[:], rhs=stat_tiles[g]["y_sum"][:], start=True, stop=True
             )
+            stat_tiles[g]["mean_ps"] = mean_ps
+
+        def negate_mean(g):
             neg_mean = work.tile([P, 1], F32, bufs=6)
             nc.vector.tensor_scalar(
-                out=neg_mean[:], in0=mean_ps[:], scalar1=-1.0, scalar2=None, op0=ALU.mult
+                out=neg_mean[:], in0=stat_tiles[g]["mean_ps"][:], scalar1=-1.0, scalar2=None, op0=ALU.mult
             )
             stat_tiles[g]["neg_mean"] = neg_mean
 
@@ -232,19 +240,22 @@ def tile_parallelretention_pb_t_kernel(tc, x, Wq, bq, kv, decay_mask, out):
             )
             nc.sync.dma_start(out=out_groups[g], in_=y[:])
 
-        def run(stage, g):
+        def run(stage, g, *args):
             if 0 <= g < GROUPS:
-                stage(g)
+                stage(g, *args)
 
         with tc.manual_schedule():
-            for k in range(-1, GROUPS + 3):
-                run(flip_x, k + 1)
+            for k in range(-2, GROUPS + 5):
                 run(quantise, k)
-                run(mean, k - 1)
-                run(variance, k - 2)
-                run(squares, k - 1)
-                run(deviation, k - 2)
-                run(finish, k - 3)
-                run(flip_kv, k + 1)
+                run(product, k - 1)
+                run(copy_kv, k + 1)
+                run(negate_mean, k - 2)
+                run(finish, k - 5)
+                run(flip_x, k + 2, (0, 1))
                 run(multiply, k)
-                run(product, k)
+                run(flip_x, k + 2, (2, 3))
+                run(flip_kv, k + 2)
+                run(mean, k - 1)
+                run(variance, k - 3)
+                run(squares, k - 2)
+                run(deviation, k - 3)

@@ -52,7 +52,12 @@ def tile_parallelretention_pb_t_kernel(tc, x, Wq, bq, kv, decay_mask, out):
         kv_tiles = []
         for g in range(GROUPS):
             x_sb = resident.tile([P, J * E], BF16, name="x_sb", bufs=GROUPS)
-            nc.sync.dma_start(out=x_sb[:], in_=x_groups[g])
+            if g == 0:
+                for j in range(J):
+                    row = slice(j * E, (j + 1) * E)
+                    nc.sync.dma_start(out=x_sb[:, row], in_=x_groups[g][:, row])
+            else:
+                nc.sync.dma_start(out=x_sb[:], in_=x_groups[g])
             x_tiles.append(x_sb)
             if g % KV_CHUNK == 0:
                 kv_sb = resident.tile([P, KV_CHUNK, J * L], BF16, name="kv_sb", bufs=GROUPS // KV_CHUNK)
@@ -102,7 +107,8 @@ def tile_parallelretention_pb_t_kernel(tc, x, Wq, bq, kv, decay_mask, out):
         code_tiles = {}
         kv_flipped_tiles = {}
         kv_t_tiles = {}
-        psum_tiles = {}
+        q_tiles = {}
+        g_tiles = {}
         y_tiles = {}
         stat_tiles = {}
 
@@ -139,7 +145,7 @@ def tile_parallelretention_pb_t_kernel(tc, x, Wq, bq, kv, decay_mask, out):
             )
             code_tiles[g] = (codes, scales)
 
-        def multiply(g):
+        def multiply_x(g):
             codes, scales = code_tiles[g]
             q_ps = psum.tile([P, J, QD], F32)
             for j in range(J):
@@ -155,15 +161,19 @@ def tile_parallelretention_pb_t_kernel(tc, x, Wq, bq, kv, decay_mask, out):
                         start=(c == 0),
                         stop=(c == PASSES - 1),
                     )
+            q_tiles[g] = q_ps
+
+        def multiply_kv(g):
             g_ps = psum.tile([P, J, QD], F32)
             for j in range(J):
                 nc.tensor.matmul(
                     out=g_ps[:, j, :], lhsT=kv_t_tiles[g][:, j, :], rhs=d_t[:], start=True, stop=True
                 )
-            psum_tiles[g] = (q_ps, g_ps)
+            g_tiles[g] = g_ps
 
         def product(g):
-            q_ps, g_ps = psum_tiles[g]
+            q_ps = q_tiles[g]
+            g_ps = g_tiles[g]
             q_biased = work.tile([P, J, QD], F32)
             nc.vector.tensor_tensor(
                 out=q_biased[:],
@@ -252,9 +262,10 @@ def tile_parallelretention_pb_t_kernel(tc, x, Wq, bq, kv, decay_mask, out):
                 run(negate_mean, k - 2)
                 run(finish, k - 5)
                 run(flip_x, k + 2, (0, 1))
-                run(multiply, k)
+                run(multiply_x, k)
                 run(flip_x, k + 2, (2, 3))
                 run(flip_kv, k + 2)
+                run(multiply_kv, k)
                 run(mean, k - 1)
                 run(variance, k - 3)
                 run(squares, k - 2)

@@ -52,12 +52,7 @@ def tile_parallelretention_pb_t_kernel(tc, x, Wq, bq, kv, decay_mask, out):
         kv_tiles = []
         for g in range(GROUPS):
             x_sb = resident.tile([P, J * E], BF16, name="x_sb", bufs=GROUPS)
-            if g == 0:
-                for j in range(J):
-                    row = slice(j * E, (j + 1) * E)
-                    nc.sync.dma_start(out=x_sb[:, row], in_=x_groups[g][:, row])
-            else:
-                nc.sync.dma_start(out=x_sb[:], in_=x_groups[g])
+            nc.sync.dma_start(out=x_sb[:], in_=x_groups[g])
             x_tiles.append(x_sb)
             if g % KV_CHUNK == 0:
                 kv_sb = resident.tile([P, KV_CHUNK, J * L], BF16, name="kv_sb", bufs=GROUPS // KV_CHUNK)
@@ -107,8 +102,7 @@ def tile_parallelretention_pb_t_kernel(tc, x, Wq, bq, kv, decay_mask, out):
         code_tiles = {}
         kv_flipped_tiles = {}
         kv_t_tiles = {}
-        q_tiles = {}
-        g_tiles = {}
+        psum_tiles = {}
         y_tiles = {}
         stat_tiles = {}
 
@@ -145,7 +139,7 @@ def tile_parallelretention_pb_t_kernel(tc, x, Wq, bq, kv, decay_mask, out):
             )
             code_tiles[g] = (codes, scales)
 
-        def multiply_x(g):
+        def multiply(g):
             codes, scales = code_tiles[g]
             q_ps = psum.tile([P, J, QD], F32)
             for j in range(J):
@@ -161,19 +155,15 @@ def tile_parallelretention_pb_t_kernel(tc, x, Wq, bq, kv, decay_mask, out):
                         start=(c == 0),
                         stop=(c == PASSES - 1),
                     )
-            q_tiles[g] = q_ps
-
-        def multiply_kv(g):
             g_ps = psum.tile([P, J, QD], F32)
             for j in range(J):
                 nc.tensor.matmul(
                     out=g_ps[:, j, :], lhsT=kv_t_tiles[g][:, j, :], rhs=d_t[:], start=True, stop=True
                 )
-            g_tiles[g] = g_ps
+            psum_tiles[g] = (q_ps, g_ps)
 
         def product(g):
-            q_ps = q_tiles[g]
-            g_ps = g_tiles[g]
+            q_ps, g_ps = psum_tiles[g]
             q_biased = work.tile([P, J, QD], F32)
             nc.vector.tensor_tensor(
                 out=q_biased[:],
@@ -240,7 +230,7 @@ def tile_parallelretention_pb_t_kernel(tc, x, Wq, bq, kv, decay_mask, out):
             rstd = work.tile([P, 1], F32, bufs=6)
             nc.vector.reciprocal(out=rstd[:], in_=stat_tiles[g]["std"][:])
             y = y_tiles[g]
-            nc.vector.tensor_scalar(
+            nc.gpsimd.tensor_scalar(
                 out=y[:],
                 in0=y[:],
                 scalar1=stat_tiles[g]["neg_mean"][:],
@@ -262,10 +252,9 @@ def tile_parallelretention_pb_t_kernel(tc, x, Wq, bq, kv, decay_mask, out):
                 run(negate_mean, k - 2)
                 run(finish, k - 5)
                 run(flip_x, k + 2, (0, 1))
-                run(multiply_x, k)
+                run(multiply, k)
                 run(flip_x, k + 2, (2, 3))
                 run(flip_kv, k + 2)
-                run(multiply_kv, k)
                 run(mean, k - 1)
                 run(variance, k - 3)
                 run(squares, k - 2)

@@ -103,6 +103,7 @@ def tile_parallelretention_pb_t_kernel(tc, x, Wq, bq, kv, decay_mask, out):
         kv_flipped_tiles = {}
         kv_t_tiles = {}
         psum_tiles = {}
+        biased_tiles = {}
         y_tiles = {}
         stat_tiles = {}
 
@@ -162,8 +163,8 @@ def tile_parallelretention_pb_t_kernel(tc, x, Wq, bq, kv, decay_mask, out):
                 )
             psum_tiles[g] = (q_ps, g_ps)
 
-        def product(g):
-            q_ps, g_ps = psum_tiles[g]
+        def add_bias(g):
+            q_ps = psum_tiles[g][0]
             q_biased = work.tile([P, J, QD], F32)
             nc.vector.tensor_tensor(
                 out=q_biased[:],
@@ -171,13 +172,16 @@ def tile_parallelretention_pb_t_kernel(tc, x, Wq, bq, kv, decay_mask, out):
                 in1=bias_rows[:].unsqueeze(1).to_broadcast([P, J, QD]),
                 op=ALU.add,
             )
+            biased_tiles[g] = q_biased
+
+        def product(g):
             y = resident.tile([P, J * QD], F32, name="y", bufs=GROUPS)
             y_sum = work.tile([P, 1], F32, bufs=6)
             nc.vector.scalar_tensor_tensor(
                 out=y[:],
-                in0=q_biased[:].rearrange("p j q -> p (j q)"),
+                in0=biased_tiles[g][:].rearrange("p j q -> p (j q)"),
                 scalar=1.0,
-                in1=g_ps[:].rearrange("p j q -> p (j q)"),
+                in1=psum_tiles[g][1][:].rearrange("p j q -> p (j q)"),
                 op0=ALU.mult,
                 op1=ALU.mult,
                 accum_out=y_sum[:],
@@ -246,6 +250,7 @@ def tile_parallelretention_pb_t_kernel(tc, x, Wq, bq, kv, decay_mask, out):
 
         with tc.manual_schedule():
             for k in range(-2, GROUPS + 5):
+                run(add_bias, k - 1)
                 run(quantise, k)
                 run(product, k - 1)
                 run(copy_kv, k + 1)

@@ -21,8 +21,9 @@ HALVES = 2
 J = 4
 GROUP_TOKENS = P * J
 GROUPS = B * L // GROUP_TOKENS
+LAST = GROUPS - 1
 SAMPLE_PARTITIONS = L // J
-KV_CHUNK = 4
+KV_CHUNK = 2
 
 FLOPS = 2 * B * L * QD * E + 2 * B * L * QD * L
 
@@ -41,18 +42,21 @@ def tile_parallelretention_pb_t_kernel(tc, x, Wq, bq, kv, decay_mask, out):
         work = ctx.enter_context(tc.tile_pool(name="work", bufs=2))
         psum = ctx.enter_context(tc.psum_pool(name="psum", bufs=1))
 
-        w_sb = consts.tile([P, E], BF16)
-        nc.scalar.dma_start(out=w_sb[:], in_=Wq)
-        d_sb = consts.tile([P, L], BF16)
-        nc.scalar.dma_start(out=d_sb[:], in_=decay_mask[0])
-        bias_rows = consts.tile([P, QD], BF16)
-        nc.scalar.dma_start(out=bias_rows[:], in_=bq.partition_broadcast(P))
-
         x_tiles = []
         kv_tiles = []
+        w_sb = consts.tile([P, E], BF16)
+        d_sb = consts.tile([P, L], BF16)
+        nc.scalar.dma_start(out=d_sb[:], in_=decay_mask[0])
         for g in range(GROUPS):
             x_sb = resident.tile([P, J * E], BF16, name="x_sb", bufs=GROUPS)
-            nc.sync.dma_start(out=x_sb[:], in_=x_groups[g])
+            if g == 0:
+                for j in range(J):
+                    cols = slice(j * E, (j + 1) * E)
+                    nc.sync.dma_start(out=x_sb[:, cols], in_=x_groups[g][:, cols])
+                    if j == 0:
+                        nc.sync.dma_start(out=w_sb[:], in_=Wq)
+            else:
+                nc.sync.dma_start(out=x_sb[:], in_=x_groups[g])
             x_tiles.append(x_sb)
             if g % KV_CHUNK == 0:
                 kv_sb = resident.tile([P, KV_CHUNK, J * L], BF16, name="kv_sb", bufs=GROUPS // KV_CHUNK)
@@ -63,6 +67,11 @@ def tile_parallelretention_pb_t_kernel(tc, x, Wq, bq, kv, decay_mask, out):
         make_identity(nc, ident_f32[:])
         ident_bf = consts.tile([P, P], BF16)
         make_identity(nc, ident_bf[:])
+        bias_row = consts.tile([P, QD], BF16)
+        nc.vector.memset(bias_row[:], 0.0)
+        nc.scalar.dma_start(out=bias_row[0:1, :], in_=bq.unsqueeze(0))
+        ones = consts.tile([P, P], BF16)
+        nc.vector.memset(ones[:], 1.0)
         sample_mean = consts.tile([P, P], F32)
         nc.vector.memset(sample_mean[:], 0.0)
         for s in range(P // SAMPLE_PARTITIONS):
@@ -84,30 +93,39 @@ def tile_parallelretention_pb_t_kernel(tc, x, Wq, bq, kv, decay_mask, out):
             copy(out=grouped_words, in_=flipped[:].rearrange("p c u r -> p c r u"))
 
         w_grouped = consts.tile([P, PASSES * QD * PACK], BF16, align_bytes=64)
-        transpose_words(
-            w_sb[:],
-            w_grouped[:].bitcast(F32).rearrange("p (c r u) -> p c r u", c=PASSES, u=HALVES),
-            nc.vector.tensor_copy,
-        )
         w_codes = consts.tile([P, PASSES * QD], U32, align_bytes=64)
         w_scales = consts.tile([P, PASSES * QD], U8, align_bytes=64)
-        nc.vector.quantize_mx(out=w_codes[:].bitcast(FP8X4), scales=w_scales[:], in_=w_grouped[:])
-
-        d_flipped = psum.tile([P, P], BF16, tag="flipped", bufs=4)
-        nc.tensor.transpose(d_flipped[:], d_sb[:], ident_bf[:])
         d_t = consts.tile([P, QD], BF16)
-        nc.vector.tensor_copy(out=d_t[:], in_=d_flipped[:])
+        bias = consts.tile([P, QD], F32)
+
+        def prepare_weights():
+            transpose_words(
+                w_sb[:],
+                w_grouped[:].bitcast(F32).rearrange("p (c r u) -> p c r u", c=PASSES, u=HALVES),
+                nc.vector.tensor_copy,
+            )
+            d_flipped = psum.tile([P, P], BF16, tag="kv_flipped", bufs=1)
+            nc.tensor.transpose(d_flipped[:], d_sb[:], ident_bf[:])
+            nc.vector.tensor_copy(out=d_t[:], in_=d_flipped[:])
+            bias_ps = psum.tile([P, QD], F32, tag="kv_flipped", bufs=1)
+            nc.tensor.matmul(out=bias_ps[:], lhsT=ones[:], rhs=bias_row[:], start=True, stop=True)
+            nc.vector.quantize_mx(out=w_codes[:].bitcast(FP8X4), scales=w_scales[:], in_=w_grouped[:])
+            nc.vector.tensor_copy(out=bias[:], in_=bias_ps[:])
 
         grouped_tiles = {}
         code_tiles = {}
         kv_flipped_tiles = {}
         kv_t_tiles = {}
-        psum_tiles = {}
+        q_tiles = {}
+        g_tiles = {}
         biased_tiles = {}
         y_tiles = {}
+        sum_tiles = {}
         stat_tiles = {}
+        neg_mean_tiles = {}
+        std_tiles = {}
 
-        def flip_x(g, rows):
+        def flip_x(g, rows=range(J)):
             if g not in grouped_tiles:
                 grouped = work.tile([P, J * PASSES * P * PACK], BF16, align_bytes=64)
                 grouped_tiles[g] = grouped
@@ -115,10 +133,11 @@ def tile_parallelretention_pb_t_kernel(tc, x, Wq, bq, kv, decay_mask, out):
                 "p (j c r u) -> p j c r u", j=J, c=PASSES, u=HALVES
             )
             for j in rows:
-                transpose_words(x_tiles[g][:, j * E : (j + 1) * E], grouped_words[:, j], nc.scalar.copy)
+                copy = nc.vector.tensor_copy if g == 0 and j % 2 == 1 else nc.scalar.copy
+                transpose_words(x_tiles[g][:, j * E : (j + 1) * E], grouped_words[:, j], copy)
 
         def flip_kv(g):
-            kv_flipped = psum.tile([P, J, P], BF16, tag="flipped", bufs=4)
+            kv_flipped = psum.tile([P, J, P], BF16, tag="kv_flipped", bufs=1)
             kv_flipped_tiles[g] = kv_flipped
             for j in range(J):
                 nc.tensor.transpose(
@@ -132,18 +151,28 @@ def tile_parallelretention_pb_t_kernel(tc, x, Wq, bq, kv, decay_mask, out):
             nc.vector.tensor_copy(out=kv_t[:], in_=kv_flipped_tiles[g][:])
             kv_t_tiles[g] = kv_t
 
-        def quantise(g):
-            codes = work.tile([P, J * PASSES * P], U32, align_bytes=64)
-            scales = work.tile([P, J * PASSES * P], U8, align_bytes=64)
-            nc.vector.quantize_mx(
-                out=codes[:].bitcast(FP8X4), scales=scales[:], in_=grouped_tiles[g][:]
-            )
-            code_tiles[g] = (codes, scales)
-
-        def multiply(g):
+        def quantise(g, rows=range(J)):
+            if g not in code_tiles:
+                codes = work.tile([P, J * PASSES * P], U32, align_bytes=64)
+                scales = work.tile([P, J * PASSES * P], U8, align_bytes=64)
+                code_tiles[g] = (codes, scales)
             codes, scales = code_tiles[g]
-            q_ps = psum.tile([P, J, QD], F32)
-            for j in range(J):
+            cols = slice(rows.start * PASSES * P, rows.stop * PASSES * P)
+            in_cols = slice(cols.start * PACK, cols.stop * PACK)
+            nc.vector.quantize_mx(
+                out=codes[:, cols].bitcast(FP8X4),
+                scales=scales[:, cols],
+                in_=grouped_tiles[g][:, in_cols],
+            )
+
+        def multiply_q(g, rows=range(J)):
+            codes, scales = code_tiles[g]
+            if g == LAST:
+                q_ps = psum.tile([P, J, QD], F32, tag="flipped", bufs=4)
+            else:
+                q_ps = psum.tile([P, J, QD], F32, tag="q", bufs=1)
+            q_tiles[g, rows.start] = q_ps
+            for j in rows:
                 for c in range(PASSES):
                     cols = slice((j * PASSES + c) * P, (j * PASSES + c + 1) * P)
                     w_cols = slice(c * QD, (c + 1) * QD)
@@ -156,88 +185,96 @@ def tile_parallelretention_pb_t_kernel(tc, x, Wq, bq, kv, decay_mask, out):
                         start=(c == 0),
                         stop=(c == PASSES - 1),
                     )
+
+        def multiply_g(g):
             g_ps = psum.tile([P, J, QD], F32)
             for j in range(J):
                 nc.tensor.matmul(
                     out=g_ps[:, j, :], lhsT=kv_t_tiles[g][:, j, :], rhs=d_t[:], start=True, stop=True
                 )
-            psum_tiles[g] = (q_ps, g_ps)
+            g_tiles[g] = g_ps
 
-        def add_bias(g):
-            q_ps = psum_tiles[g][0]
-            q_biased = work.tile([P, J, QD], F32)
+        def add_bias(g, rows=range(J)):
+            if g not in biased_tiles:
+                q_biased = work.tile([P, J, QD], F32)
+                biased_tiles[g] = q_biased
+            part = slice(rows.start, rows.stop)
             nc.vector.tensor_tensor(
-                out=q_biased[:],
-                in0=q_ps[:],
-                in1=bias_rows[:].unsqueeze(1).to_broadcast([P, J, QD]),
+                out=biased_tiles[g][:, part, :],
+                in0=q_tiles[g, rows.start][:, part, :],
+                in1=bias[:].unsqueeze(1).to_broadcast([P, len(rows), QD]),
                 op=ALU.add,
             )
-            biased_tiles[g] = q_biased
 
-        def product(g):
-            y = resident.tile([P, J * QD], F32, name="y", bufs=GROUPS)
-            y_sum = work.tile([P, 1], F32, bufs=6)
+        def sums(round_index):
+            if round_index not in sum_tiles:
+                y_and_squares = work.tile([P, 3], F32, bufs=5)
+                sum_tiles[round_index] = y_and_squares
+            return sum_tiles[round_index]
+
+        def product(g, rows=range(J), column=0):
+            if g not in y_tiles:
+                y = resident.tile([P, J * QD], F32, name="y", bufs=GROUPS)
+                y_tiles[g] = y
+            part = slice(rows.start, rows.stop)
+            cols = slice(rows.start * QD, rows.stop * QD)
             nc.vector.scalar_tensor_tensor(
-                out=y[:],
-                in0=biased_tiles[g][:].rearrange("p j q -> p (j q)"),
+                out=y_tiles[g][:, cols],
+                in0=biased_tiles[g][:, part, :].rearrange("p j q -> p (j q)"),
                 scalar=1.0,
-                in1=psum_tiles[g][1][:].rearrange("p j q -> p (j q)"),
+                in1=g_tiles[g][:, part, :].rearrange("p j q -> p (j q)"),
                 op0=ALU.mult,
                 op1=ALU.mult,
-                accum_out=y_sum[:],
+                accum_out=sums(g + 1)[:, column : column + 1],
             )
-            y_tiles[g] = y
-            stat_tiles[g] = {"y_sum": y_sum}
-
-        def mean(g):
-            mean_ps = psum.tile([P, 1], F32)
-            nc.tensor.matmul(
-                out=mean_ps[:], lhsT=sample_mean[:], rhs=stat_tiles[g]["y_sum"][:], start=True, stop=True
-            )
-            stat_tiles[g]["mean_ps"] = mean_ps
-
-        def negate_mean(g):
-            neg_mean = work.tile([P, 1], F32, bufs=6)
-            nc.vector.tensor_scalar(
-                out=neg_mean[:], in0=stat_tiles[g]["mean_ps"][:], scalar1=-1.0, scalar2=None, op0=ALU.mult
-            )
-            stat_tiles[g]["neg_mean"] = neg_mean
 
         def squares(g):
             squared = work.tile([P, J * QD], BF16, bufs=2)
-            sq_sum = work.tile([P, 1], F32, bufs=6)
             nc.scalar.activation(
                 out=squared[:],
                 in_=y_tiles[g][:],
                 func=ACT.Square,
-                bias=stat_tiles[g]["neg_mean"][:],
+                bias=neg_mean_tiles[g][:],
                 scale=1.0,
-                accum_out=sq_sum[:],
+                accum_out=sums(g + 3)[:, 1:2],
             )
-            stat_tiles[g]["sq_sum"] = sq_sum
 
-        def variance(g):
-            var_ps = psum.tile([P, 1], F32)
+        def statistics(r):
+            stats = psum.tile([P, 2], F32)
+            lo = 0 if r - 1 <= LAST else 1
+            hi = 2 if r - 3 >= 0 else 1
             nc.tensor.matmul(
-                out=var_ps[:], lhsT=sample_mean[:], rhs=stat_tiles[g]["sq_sum"][:], start=True, stop=True
+                out=stats[:, lo:hi], lhsT=sample_mean[:], rhs=sums(r)[:, lo:hi], start=True, stop=r - 1 != LAST
             )
-            stat_tiles[g]["var_ps"] = var_ps
+            if r - 1 == LAST:
+                nc.tensor.matmul(
+                    out=stats[:, 0:1], lhsT=sample_mean[:], rhs=sums(r)[:, 2:3], start=False, stop=True
+                )
+            stat_tiles[r] = stats
+
+        def negate_mean(g):
+            neg_mean = work.tile([P, 1], F32, bufs=6)
+            nc.vector.tensor_scalar(
+                out=neg_mean[:], in0=stat_tiles[g + 1][:, 0:1], scalar1=-1.0, scalar2=None, op0=ALU.mult
+            )
+            neg_mean_tiles[g] = neg_mean
 
         def deviation(g):
             std = work.tile([P, 1], F32, bufs=6)
             nc.scalar.activation(
-                out=std[:], in_=stat_tiles[g]["var_ps"][:], func=ACT.Sqrt, bias=eps[:], scale=1.0
+                out=std[:], in_=stat_tiles[g + 3][:, 1:2], func=ACT.Sqrt, bias=eps[:], scale=1.0
             )
-            stat_tiles[g]["std"] = std
+            std_tiles[g] = std
 
         def finish(g):
             rstd = work.tile([P, 1], F32, bufs=6)
-            nc.vector.reciprocal(out=rstd[:], in_=stat_tiles[g]["std"][:])
+            nc.vector.reciprocal(out=rstd[:], in_=std_tiles[g][:])
             y = y_tiles[g]
-            nc.gpsimd.tensor_scalar(
+            engine = nc.vector if g == LAST else nc.gpsimd
+            engine.tensor_scalar(
                 out=y[:],
                 in0=y[:],
-                scalar1=stat_tiles[g]["neg_mean"][:],
+                scalar1=neg_mean_tiles[g][:],
                 scalar2=rstd[:],
                 op0=ALU.add,
                 op1=ALU.mult,
@@ -248,19 +285,42 @@ def tile_parallelretention_pb_t_kernel(tc, x, Wq, bq, kv, decay_mask, out):
             if 0 <= g < GROUPS:
                 stage(g, *args)
 
+        first_half, second_half = range(0, J // 2), range(J // 2, J)
         with tc.manual_schedule():
-            for k in range(-2, GROUPS + 5):
-                run(add_bias, k - 1)
-                run(quantise, k)
-                run(product, k - 1)
-                run(copy_kv, k + 1)
+            flip_x(0, range(0, 1))
+            prepare_weights()
+            flip_x(0, range(1, J))
+            flip_kv(0)
+            copy_kv(0)
+            quantise(0)
+            flip_x(1)
+            flip_kv(1)
+            for k in range(GROUPS + 4):
+                if k == LAST + 1:
+                    add_bias(LAST, first_half)
+                    add_bias(LAST, second_half)
+                    product(LAST, first_half, 0)
+                    product(LAST, second_half, 2)
+                else:
+                    run(add_bias, k - 1)
+                    run(copy_kv, k + 1)
+                    run(product, k - 1)
                 run(negate_mean, k - 2)
-                run(finish, k - 5)
-                run(flip_x, k + 2, (0, 1))
-                run(multiply, k)
-                run(flip_x, k + 2, (2, 3))
+                if k + 1 == LAST:
+                    quantise(LAST, first_half)
+                    quantise(LAST, second_half)
+                else:
+                    run(quantise, k + 1)
+                run(finish, k - 4)
+                run(flip_x, k + 2)
                 run(flip_kv, k + 2)
-                run(mean, k - 1)
-                run(variance, k - 3)
+                if k == LAST:
+                    multiply_q(LAST, first_half)
+                    multiply_q(LAST, second_half)
+                else:
+                    run(multiply_q, k)
+                run(multiply_g, k)
+                if 1 <= k <= GROUPS + 2:
+                    statistics(k)
                 run(squares, k - 2)
                 run(deviation, k - 3)

@@ -49,16 +49,14 @@ def tile_parallelretention_pb_t_kernel(tc, x, Wq, bq, kv, decay_mask, out):
         nc.scalar.dma_start(out=d_sb[:], in_=decay_mask[0])
         for g in range(GROUPS):
             x_sb = resident.tile([P, J * E], BF16, name="x_sb", bufs=GROUPS)
-            if g == 0:
-                for j in range(J):
-                    cols = slice(j * E, (j + 1) * E)
-                    nc.sync.dma_start(out=x_sb[:, cols], in_=x_groups[g][:, cols])
-                    if j == 0:
-                        nc.sync.dma_start(out=w_sb[:], in_=Wq)
-            else:
-                nc.sync.dma_start(out=x_sb[:], in_=x_groups[g])
+            pieces = {0: 4, 1: 2, 2: 2}.get(g, 1)
+            for i in range(pieces):
+                cols = slice(i * J * E // pieces, (i + 1) * J * E // pieces)
+                nc.sync.dma_start(out=x_sb[:, cols], in_=x_groups[g][:, cols])
+                if g == 0 and i == 1:
+                    nc.sync.dma_start(out=w_sb[:], in_=Wq)
             x_tiles.append(x_sb)
-            if g % KV_CHUNK == 0:
+            if g == 1 or (g > 0 and g % KV_CHUNK == 0):
                 kv_sb = resident.tile([P, KV_CHUNK, J * L], BF16, name="kv_sb", bufs=GROUPS // KV_CHUNK)
                 nc.sync.dma_start(out=kv_sb[:], in_=kv_chunks[g // KV_CHUNK])
                 kv_tiles.append(kv_sb)
@@ -72,17 +70,17 @@ def tile_parallelretention_pb_t_kernel(tc, x, Wq, bq, kv, decay_mask, out):
         nc.scalar.dma_start(out=bias_row[0:1, :], in_=bq.unsqueeze(0))
         ones = consts.tile([P, P], BF16)
         nc.vector.memset(ones[:], 1.0)
-        sample_mean = consts.tile([P, P], F32)
-        nc.vector.memset(sample_mean[:], 0.0)
+        neg_sample_mean = consts.tile([P, P], F32)
+        nc.vector.memset(neg_sample_mean[:], 0.0)
         for s in range(P // SAMPLE_PARTITIONS):
             rows = slice(s * SAMPLE_PARTITIONS, (s + 1) * SAMPLE_PARTITIONS)
-            nc.vector.memset(sample_mean[rows, rows], 1.0 / (L * QD))
+            nc.vector.memset(neg_sample_mean[rows, rows], -1.0 / (L * QD))
         one = consts.tile([P, 1], F32)
         nc.vector.memset(one[:], 1.0)
         eps = consts.tile([P, 1], F32)
         nc.vector.memset(eps[:], EPS)
         warm = consts.tile([P, 1], F32)
-        nc.scalar.activation(out=warm[:], in_=one[:], func=ACT.Sqrt)
+        nc.scalar.activation(out=warm[:], in_=one[:], func=ACT.Abs_reciprocal_sqrt)
 
         def transpose_words(rows_bf16, grouped_words, copy):
             words = rows_bf16.bitcast(F32).rearrange("p (c u w) -> p c u w", c=PASSES, u=HALVES)
@@ -104,11 +102,11 @@ def tile_parallelretention_pb_t_kernel(tc, x, Wq, bq, kv, decay_mask, out):
                 w_grouped[:].bitcast(F32).rearrange("p (c r u) -> p c r u", c=PASSES, u=HALVES),
                 nc.vector.tensor_copy,
             )
-            d_flipped = psum.tile([P, P], BF16, tag="kv_flipped", bufs=1)
+            d_flipped = psum.tile([P, P], BF16, tag="g", bufs=1)
             nc.tensor.transpose(d_flipped[:], d_sb[:], ident_bf[:])
-            nc.vector.tensor_copy(out=d_t[:], in_=d_flipped[:])
-            bias_ps = psum.tile([P, QD], F32, tag="kv_flipped", bufs=1)
+            bias_ps = psum.tile([P, QD], F32, tag="stats", bufs=1)
             nc.tensor.matmul(out=bias_ps[:], lhsT=ones[:], rhs=bias_row[:], start=True, stop=True)
+            nc.vector.tensor_copy(out=d_t[:], in_=d_flipped[:])
             nc.vector.quantize_mx(out=w_codes[:].bitcast(FP8X4), scales=w_scales[:], in_=w_grouped[:])
             nc.vector.tensor_copy(out=bias[:], in_=bias_ps[:])
 
@@ -121,9 +119,10 @@ def tile_parallelretention_pb_t_kernel(tc, x, Wq, bq, kv, decay_mask, out):
         biased_tiles = {}
         y_tiles = {}
         sum_tiles = {}
-        stat_tiles = {}
-        neg_mean_tiles = {}
-        std_tiles = {}
+        neg_mean_psums = {}
+        neg_variance_psums = {}
+        neg_means = {}
+        rstds = {}
 
         def flip_x(g, rows=range(J)):
             if g not in grouped_tiles:
@@ -133,8 +132,7 @@ def tile_parallelretention_pb_t_kernel(tc, x, Wq, bq, kv, decay_mask, out):
                 "p (j c r u) -> p j c r u", j=J, c=PASSES, u=HALVES
             )
             for j in rows:
-                copy = nc.vector.tensor_copy if g == 0 and j % 2 == 1 else nc.scalar.copy
-                transpose_words(x_tiles[g][:, j * E : (j + 1) * E], grouped_words[:, j], copy)
+                transpose_words(x_tiles[g][:, j * E : (j + 1) * E], grouped_words[:, j], nc.scalar.copy)
 
         def flip_kv(g):
             kv_flipped = psum.tile([P, J, P], BF16, tag="kv_flipped", bufs=1)
@@ -187,7 +185,10 @@ def tile_parallelretention_pb_t_kernel(tc, x, Wq, bq, kv, decay_mask, out):
                     )
 
         def multiply_g(g):
-            g_ps = psum.tile([P, J, QD], F32)
+            if g == LAST:
+                g_ps = psum.tile([P, J, QD], F32, tag="flipped", bufs=4)
+            else:
+                g_ps = psum.tile([P, J, QD], F32, tag="g", bufs=1)
             for j in range(J):
                 nc.tensor.matmul(
                     out=g_ps[:, j, :], lhsT=kv_t_tiles[g][:, j, :], rhs=d_t[:], start=True, stop=True
@@ -206,27 +207,85 @@ def tile_parallelretention_pb_t_kernel(tc, x, Wq, bq, kv, decay_mask, out):
                 op=ALU.add,
             )
 
-        def sums(round_index):
-            if round_index not in sum_tiles:
-                y_and_squares = work.tile([P, 3], F32, bufs=5)
-                sum_tiles[round_index] = y_and_squares
-            return sum_tiles[round_index]
+        def pair(g):
+            return (g + 1) // 2
 
-        def product(g, rows=range(J), column=0):
-            if g not in y_tiles:
-                y = resident.tile([P, J * QD], F32, name="y", bufs=GROUPS)
-                y_tiles[g] = y
-            part = slice(rows.start, rows.stop)
-            cols = slice(rows.start * QD, rows.stop * QD)
+        def sums(i):
+            if i not in sum_tiles:
+                sum_columns = work.tile([P, 4], F32, bufs=5)
+                sum_tiles[i] = sum_columns
+            return sum_tiles[i]
+
+        def y_sum(g):
+            column = 1 if g % 2 == 1 else 2
+            return sums(pair(g))[:, column : column + 1]
+
+        def square_sum(g):
+            column = 0 if g % 2 == 1 else 3
+            return sums(pair(g) + 1)[:, column : column + 1]
+
+        def product(g):
+            y = resident.tile([P, J * QD], F32, name="y", bufs=GROUPS)
             nc.vector.scalar_tensor_tensor(
-                out=y_tiles[g][:, cols],
-                in0=biased_tiles[g][:, part, :].rearrange("p j q -> p (j q)"),
+                out=y[:],
+                in0=biased_tiles[g][:].rearrange("p j q -> p (j q)"),
                 scalar=1.0,
-                in1=g_tiles[g][:, part, :].rearrange("p j q -> p (j q)"),
+                in1=g_tiles[g][:].rearrange("p j q -> p (j q)"),
                 op0=ALU.mult,
                 op1=ALU.mult,
-                accum_out=sums(g + 1)[:, column : column + 1],
+                accum_out=y_sum(g),
             )
+            y_tiles[g] = y
+
+        def statistics(i):
+            stats = psum.tile([P, 4], F32, tag="stats", bufs=1)
+            columns = slice({0: 2, 1: 1}.get(i, 0), 3 if i == 0 else 4)
+            nc.tensor.matmul(
+                out=stats[:, columns], lhsT=neg_sample_mean[:], rhs=sums(i)[:, columns], start=True, stop=True
+            )
+            neg_mean_psums[i] = stats
+            neg_variance_psums[i - 1] = stats
+
+        def pair_means(i):
+            neg_mean = work.tile([P, 2], F32, bufs=4)
+            lo = 1 if i == 0 else 0
+            nc.scalar.copy(out=neg_mean[:, lo:2], in_=neg_mean_psums[i][:, 1 + lo : 3])
+            neg_means[2 * i - 1] = neg_mean[:, 0:1]
+            neg_means[2 * i] = neg_mean[:, 1:2]
+
+        def inverse_deviation(out, neg_variance):
+            nc.scalar.activation(
+                out=out, in_=neg_variance, func=ACT.Abs_reciprocal_sqrt, bias=eps[:], scale=-1.0
+            )
+
+        def pair_deviations(i):
+            rstd = work.tile([P, 2], F32, bufs=4)
+            lo = 1 if i == 0 else 0
+            inverse_deviation(rstd[:, lo:2], neg_variance_psums[i][:, 3 * lo : 4 : 3])
+            rstds[2 * i - 1] = rstd[:, 0:1]
+            rstds[2 * i] = rstd[:, 1:2]
+
+        def mean(g):
+            neg_mean_ps = psum.tile([P, 1], F32, tag="flipped", bufs=4)
+            nc.tensor.matmul(out=neg_mean_ps[:], lhsT=neg_sample_mean[:], rhs=y_sum(g), start=True, stop=True)
+            neg_mean_psums[g, 1] = neg_mean_ps
+
+        def copy_mean(g):
+            neg_mean_of_one = work.tile([P, 1], F32, bufs=4)
+            nc.scalar.copy(out=neg_mean_of_one[:], in_=neg_mean_psums[g, 1][:])
+            neg_means[g] = neg_mean_of_one[:]
+
+        def variance(g):
+            neg_variance_ps = psum.tile([P, 1], F32, tag="flipped", bufs=4)
+            nc.tensor.matmul(
+                out=neg_variance_ps[:], lhsT=neg_sample_mean[:], rhs=square_sum(g), start=True, stop=True
+            )
+            neg_variance_psums[g, 1] = neg_variance_ps
+
+        def deviation(g):
+            rstd_of_one = work.tile([P, 1], F32, bufs=4)
+            inverse_deviation(rstd_of_one[:], neg_variance_psums[g, 1][:])
+            rstds[g] = rstd_of_one[:]
 
         def squares(g):
             squared = work.tile([P, J * QD], BF16, bufs=2)
@@ -234,50 +293,16 @@ def tile_parallelretention_pb_t_kernel(tc, x, Wq, bq, kv, decay_mask, out):
                 out=squared[:],
                 in_=y_tiles[g][:],
                 func=ACT.Square,
-                bias=neg_mean_tiles[g][:],
+                bias=neg_means[g],
                 scale=1.0,
-                accum_out=sums(g + 3)[:, 1:2],
+                accum_out=square_sum(g),
             )
-
-        def statistics(r):
-            stats = psum.tile([P, 2], F32)
-            lo = 0 if r - 1 <= LAST else 1
-            hi = 2 if r - 3 >= 0 else 1
-            nc.tensor.matmul(
-                out=stats[:, lo:hi], lhsT=sample_mean[:], rhs=sums(r)[:, lo:hi], start=True, stop=r - 1 != LAST
-            )
-            if r - 1 == LAST:
-                nc.tensor.matmul(
-                    out=stats[:, 0:1], lhsT=sample_mean[:], rhs=sums(r)[:, 2:3], start=False, stop=True
-                )
-            stat_tiles[r] = stats
-
-        def negate_mean(g):
-            neg_mean = work.tile([P, 1], F32, bufs=6)
-            nc.vector.tensor_scalar(
-                out=neg_mean[:], in0=stat_tiles[g + 1][:, 0:1], scalar1=-1.0, scalar2=None, op0=ALU.mult
-            )
-            neg_mean_tiles[g] = neg_mean
-
-        def deviation(g):
-            std = work.tile([P, 1], F32, bufs=6)
-            nc.scalar.activation(
-                out=std[:], in_=stat_tiles[g + 3][:, 1:2], func=ACT.Sqrt, bias=eps[:], scale=1.0
-            )
-            std_tiles[g] = std
 
         def finish(g):
-            rstd = work.tile([P, 1], F32, bufs=6)
-            nc.vector.reciprocal(out=rstd[:], in_=std_tiles[g][:])
             y = y_tiles[g]
             engine = nc.vector if g == LAST else nc.gpsimd
             engine.tensor_scalar(
-                out=y[:],
-                in0=y[:],
-                scalar1=neg_mean_tiles[g][:],
-                scalar2=rstd[:],
-                op0=ALU.add,
-                op1=ALU.mult,
+                out=y[:], in0=y[:], scalar1=neg_means[g], scalar2=rstds[g], op0=ALU.add, op1=ALU.mult
             )
             nc.sync.dma_start(out=out_groups[g], in_=y[:])
 
@@ -287,40 +312,82 @@ def tile_parallelretention_pb_t_kernel(tc, x, Wq, bq, kv, decay_mask, out):
 
         first_half, second_half = range(0, J // 2), range(J // 2, J)
         with tc.manual_schedule():
-            flip_x(0, range(0, 1))
+            flip_x(0, first_half)
             prepare_weights()
-            flip_x(0, range(1, J))
+            flip_x(0, second_half)
+            quantise(0, first_half)
+            quantise(0, second_half)
+            flip_x(1)
+            multiply_q(0)
             flip_kv(0)
             copy_kv(0)
-            quantise(0)
-            flip_x(1)
+            flip_x(2, first_half)
+            multiply_g(0)
             flip_kv(1)
-            for k in range(GROUPS + 4):
-                if k == LAST + 1:
-                    add_bias(LAST, first_half)
-                    add_bias(LAST, second_half)
-                    product(LAST, first_half, 0)
-                    product(LAST, second_half, 2)
-                else:
-                    run(add_bias, k - 1)
-                    run(copy_kv, k + 1)
-                    run(product, k - 1)
-                run(negate_mean, k - 2)
+            flip_x(2, second_half)
+            add_bias(0)
+            copy_kv(1)
+            product(0)
+            quantise(1)
+            flip_kv(2)
+            for k in range(1, LAST):
+                if k > 1:
+                    add_bias(k - 1)
+                copy_kv(k + 1)
+                if k > 1:
+                    product(k - 1)
                 if k + 1 == LAST:
                     quantise(LAST, first_half)
                     quantise(LAST, second_half)
                 else:
-                    run(quantise, k + 1)
-                run(finish, k - 4)
-                run(flip_x, k + 2)
+                    quantise(k + 1)
+                if k % 2 == 1:
+                    run(squares, k - 3)
+                run(flip_x, k + 2, first_half)
+                if k % 2 == 0:
+                    pair_means(k // 2 - 1)
+                    if k >= 4:
+                        pair_deviations(k // 2 - 2)
+                        run(finish, k - 5)
+                        finish(k - 4)
+                run(flip_x, k + 2, second_half)
+                if k % 2 == 0:
+                    run(squares, k - 3)
                 run(flip_kv, k + 2)
-                if k == LAST:
-                    multiply_q(LAST, first_half)
-                    multiply_q(LAST, second_half)
-                else:
-                    run(multiply_q, k)
-                run(multiply_g, k)
-                if 1 <= k <= GROUPS + 2:
-                    statistics(k)
-                run(squares, k - 2)
-                run(deviation, k - 3)
+                multiply_q(k)
+                multiply_g(k)
+                if k % 2 == 1:
+                    statistics((k - 1) // 2)
+            mean(LAST - 2)
+            squares(LAST - 3)
+            copy_mean(LAST - 2)
+            multiply_q(LAST, first_half)
+            multiply_q(LAST, second_half)
+            multiply_g(LAST)
+            add_bias(LAST - 1)
+            add_bias(LAST, first_half)
+            product(LAST - 1)
+            add_bias(LAST, second_half)
+            variance(LAST - 4)
+            variance(LAST - 3)
+            mean(LAST - 1)
+            squares(LAST - 2)
+            deviation(LAST - 4)
+            finish(LAST - 4)
+            deviation(LAST - 3)
+            finish(LAST - 3)
+            copy_mean(LAST - 1)
+            product(LAST)
+            variance(LAST - 2)
+            mean(LAST)
+            squares(LAST - 1)
+            copy_mean(LAST)
+            deviation(LAST - 2)
+            finish(LAST - 2)
+            squares(LAST)
+            variance(LAST - 1)
+            deviation(LAST - 1)
+            finish(LAST - 1)
+            variance(LAST)
+            deviation(LAST)
+            finish(LAST)

@@ -49,7 +49,7 @@ def tile_parallelretention_pb_t_kernel(tc, x, Wq, bq, kv, decay_mask, out):
         nc.scalar.dma_start(out=d_sb[:], in_=decay_mask[0])
         for g in range(GROUPS):
             x_sb = resident.tile([P, J * E], BF16, name="x_sb", bufs=GROUPS)
-            pieces = {0: 4, 1: 2, 2: 2}.get(g, 1)
+            pieces = {0: 4}.get(g, 1)
             for i in range(pieces):
                 cols = slice(i * J * E // pieces, (i + 1) * J * E // pieces)
                 nc.sync.dma_start(out=x_sb[:, cols], in_=x_groups[g][:, cols])
@@ -300,7 +300,7 @@ def tile_parallelretention_pb_t_kernel(tc, x, Wq, bq, kv, decay_mask, out):
 
         def finish(g):
             y = y_tiles[g]
-            engine = nc.vector if g == LAST else nc.gpsimd
+            engine = nc.vector if g >= LAST - 2 else nc.gpsimd
             engine.tensor_scalar(
                 out=y[:], in0=y[:], scalar1=neg_means[g], scalar2=rstds[g], op0=ALU.add, op1=ALU.mult
             )
@@ -325,10 +325,11 @@ def tile_parallelretention_pb_t_kernel(tc, x, Wq, bq, kv, decay_mask, out):
             multiply_g(0)
             flip_kv(1)
             flip_x(2, second_half)
+            quantise(1)
             add_bias(0)
             copy_kv(1)
             product(0)
-            quantise(1)
+            multiply_q(1)
             flip_kv(2)
             for k in range(1, LAST):
                 if k > 1:
@@ -354,7 +355,8 @@ def tile_parallelretention_pb_t_kernel(tc, x, Wq, bq, kv, decay_mask, out):
                 if k % 2 == 0:
                     run(squares, k - 3)
                 run(flip_kv, k + 2)
-                multiply_q(k)
+                if k > 1:
+                    multiply_q(k)
                 multiply_g(k)
                 if k % 2 == 1:
                     statistics((k - 1) // 2)

from contextlib import ExitStack

import concourse.mybir as mybir
from concourse.masks import make_identity

F32 = mybir.dt.float32
BF16 = mybir.dt.bfloat16
U32 = mybir.dt.uint32
U8 = mybir.dt.uint8
FP8X4 = mybir.dt.float8_e4m3fn_x4
ALU = mybir.AluOpType
ACT = mybir.ActivationFunctionType

P = 128
B, L, E, QD = 64, 128, 1024, 128
EPS = 1e-5
PACK = 4
K_PASS = P * PACK
PASSES = E // K_PASS
HALVES = 2
J = 4
GROUP_TOKENS = P * J
GROUPS = B * L // GROUP_TOKENS
LAST = GROUPS - 1
SAMPLE_PARTITIONS = L // J
KV_CHUNK = 2

FLOPS = 2 * B * L * QD * E + 2 * B * L * QD * L


def tile_parallelretention_pb_t_kernel(tc, x, Wq, bq, kv, decay_mask, out):
    nc = tc.nc
    x_groups = x.rearrange("n h l e -> (n h l) e").rearrange("(g p j) e -> g p (j e)", p=P, j=J)
    kv_chunks = kv.rearrange("n h l k -> (n h l) k").rearrange(
        "(a g p j) k -> a p g (j k)", g=KV_CHUNK, p=P, j=J
    )
    out_groups = out.rearrange("n l q -> (n l) q").rearrange("(g p j) q -> g p (j q)", p=P, j=J)

    with ExitStack() as ctx:
        consts = ctx.enter_context(tc.tile_pool(name="consts", bufs=1))
        resident = ctx.enter_context(tc.tile_pool(name="resident", bufs=1))
        work = ctx.enter_context(tc.tile_pool(name="work", bufs=2))
        psum = ctx.enter_context(tc.psum_pool(name="psum", bufs=1))

        x_tiles = []
        kv_tiles = []
        w_sb = consts.tile([P, E], BF16)
        d_sb = consts.tile([P, L], BF16)
        nc.scalar.dma_start(out=d_sb[:], in_=decay_mask[0])
        for g in range(GROUPS):
            x_sb = resident.tile([P, J * E], BF16, name="x_sb", bufs=GROUPS)
            pieces = {0: 4}.get(g, 1)
            for i in range(pieces):
                cols = slice(i * J * E // pieces, (i + 1) * J * E // pieces)
                nc.sync.dma_start(out=x_sb[:, cols], in_=x_groups[g][:, cols])
                if g == 0 and i == 1:
                    nc.sync.dma_start(out=w_sb[:], in_=Wq)
            x_tiles.append(x_sb)
            if g == 1 or (g > 0 and g % KV_CHUNK == 0):
                kv_sb = resident.tile([P, KV_CHUNK, J * L], BF16, name="kv_sb", bufs=GROUPS // KV_CHUNK)
                nc.sync.dma_start(out=kv_sb[:], in_=kv_chunks[g // KV_CHUNK])
                kv_tiles.append(kv_sb)

        ident_f32 = consts.tile([P, P], F32)
        make_identity(nc, ident_f32[:])
        ident_bf = consts.tile([P, P], BF16)
        make_identity(nc, ident_bf[:])
        bias_row = consts.tile([P, QD], BF16)
        nc.vector.memset(bias_row[:], 0.0)
        nc.scalar.dma_start(out=bias_row[0:1, :], in_=bq.unsqueeze(0))
        ones = consts.tile([P, P], BF16)
        nc.vector.memset(ones[:], 1.0)
        neg_sample_mean = consts.tile([P, P], F32)
        nc.vector.memset(neg_sample_mean[:], 0.0)
        for s in range(P // SAMPLE_PARTITIONS):
            rows = slice(s * SAMPLE_PARTITIONS, (s + 1) * SAMPLE_PARTITIONS)
            nc.vector.memset(neg_sample_mean[rows, rows], -1.0 / (L * QD))
        one = consts.tile([P, 1], F32)
        nc.vector.memset(one[:], 1.0)
        eps = consts.tile([P, 1], F32)
        nc.vector.memset(eps[:], EPS)
        warm = consts.tile([P, 1], F32)
        nc.scalar.activation(out=warm[:], in_=one[:], func=ACT.Abs_reciprocal_sqrt)

        def transpose_words(rows_bf16, grouped_words, copy):
            words = rows_bf16.bitcast(F32).rearrange("p (c u w) -> p c u w", c=PASSES, u=HALVES)
            flipped = psum.tile([P, PASSES, HALVES, P], F32, tag="flipped", bufs=4)
            for c in range(PASSES):
                for u in range(HALVES):
                    nc.tensor.transpose(flipped[:, c, u, :], words[:, c, u, :], ident_f32[:])
            copy(out=grouped_words, in_=flipped[:].rearrange("p c u r -> p c r u"))

        w_grouped = consts.tile([P, PASSES * QD * PACK], BF16, align_bytes=64)
        w_codes = consts.tile([P, PASSES * QD], U32, align_bytes=64)
        w_scales = consts.tile([P, PASSES * QD], U8, align_bytes=64)
        d_t = consts.tile([P, QD], BF16)
        bias = consts.tile([P, QD], F32)

        def prepare_weights():
            transpose_words(
                w_sb[:],
                w_grouped[:].bitcast(F32).rearrange("p (c r u) -> p c r u", c=PASSES, u=HALVES),
                nc.vector.tensor_copy,
            )
            d_flipped = psum.tile([P, P], BF16, tag="g", bufs=1)
            nc.tensor.transpose(d_flipped[:], d_sb[:], ident_bf[:])
            bias_ps = psum.tile([P, QD], F32, tag="stats", bufs=1)
            nc.tensor.matmul(out=bias_ps[:], lhsT=ones[:], rhs=bias_row[:], start=True, stop=True)
            nc.vector.tensor_copy(out=d_t[:], in_=d_flipped[:])
            nc.vector.quantize_mx(out=w_codes[:].bitcast(FP8X4), scales=w_scales[:], in_=w_grouped[:])
            nc.vector.tensor_copy(out=bias[:], in_=bias_ps[:])

        grouped_tiles = {}
        code_tiles = {}
        kv_flipped_tiles = {}
        kv_t_tiles = {}
        q_tiles = {}
        g_tiles = {}
        biased_tiles = {}
        y_tiles = {}
        sum_tiles = {}
        neg_mean_psums = {}
        neg_variance_psums = {}
        neg_means = {}
        rstds = {}

        def flip_x(g, rows=range(J)):
            if g not in grouped_tiles:
                grouped = work.tile([P, J * PASSES * P * PACK], BF16, align_bytes=64)
                grouped_tiles[g] = grouped
            grouped_words = grouped_tiles[g][:].bitcast(F32).rearrange(
                "p (j c r u) -> p j c r u", j=J, c=PASSES, u=HALVES
            )
            for j in rows:
                transpose_words(x_tiles[g][:, j * E : (j + 1) * E], grouped_words[:, j], nc.scalar.copy)

        def flip_kv(g):
            kv_flipped = psum.tile([P, J, P], BF16, tag="kv_flipped", bufs=1)
            kv_flipped_tiles[g] = kv_flipped
            for j in range(J):
                nc.tensor.transpose(
                    kv_flipped[:, j, :],
                    kv_tiles[g // KV_CHUNK][:, g % KV_CHUNK, j * L : (j + 1) * L],
                    ident_bf[:],
                )

        def copy_kv(g):
            kv_t = work.tile([P, J, P], BF16, bufs=3)
            nc.vector.tensor_copy(out=kv_t[:], in_=kv_flipped_tiles[g][:])
            kv_t_tiles[g] = kv_t

        def quantise(g, rows=range(J)):
            if g not in code_tiles:
                codes = work.tile([P, J * PASSES * P], U32, align_bytes=64)
                scales = work.tile([P, J * PASSES * P], U8, align_bytes=64)
                code_tiles[g] = (codes, scales)
            codes, scales = code_tiles[g]
            cols = slice(rows.start * PASSES * P, rows.stop * PASSES * P)
            in_cols = slice(cols.start * PACK, cols.stop * PACK)
            nc.vector.quantize_mx(
                out=codes[:, cols].bitcast(FP8X4),
                scales=scales[:, cols],
                in_=grouped_tiles[g][:, in_cols],
            )

        def multiply_q(g, rows=range(J)):
            codes, scales = code_tiles[g]
            if g == LAST:
                q_ps = psum.tile([P, J, QD], F32, tag="flipped", bufs=4)
            else:
                q_ps = psum.tile([P, J, QD], F32, tag="q", bufs=1)
            q_tiles[g, rows.start] = q_ps
            for j in rows:
                for c in range(PASSES):
                    cols = slice((j * PASSES + c) * P, (j * PASSES + c + 1) * P)
                    w_cols = slice(c * QD, (c + 1) * QD)
                    nc.tensor.matmul_mx(
                        out=q_ps[:, j, :],
                        lhsT=codes[:, cols].bitcast(FP8X4),
                        lhsT_scale=scales[:, cols],
                        rhs=w_codes[:, w_cols].bitcast(FP8X4),
                        rhs_scale=w_scales[:, w_cols],
                        start=(c == 0),
                        stop=(c == PASSES - 1),
                    )

        def multiply_g(g):
            if g == LAST:
                g_ps = psum.tile([P, J, QD], F32, tag="flipped", bufs=4)
            else:
                g_ps = psum.tile([P, J, QD], F32, tag="g", bufs=1)
            for j in range(J):
                nc.tensor.matmul(
                    out=g_ps[:, j, :], lhsT=kv_t_tiles[g][:, j, :], rhs=d_t[:], start=True, stop=True
                )
            g_tiles[g] = g_ps

        def add_bias(g, rows=range(J)):
            if g not in biased_tiles:
                q_biased = work.tile([P, J, QD], F32)
                biased_tiles[g] = q_biased
            part = slice(rows.start, rows.stop)
            nc.vector.tensor_tensor(
                out=biased_tiles[g][:, part, :],
                in0=q_tiles[g, rows.start][:, part, :],
                in1=bias[:].unsqueeze(1).to_broadcast([P, len(rows), QD]),
                op=ALU.add,
            )

        def pair(g):
            return (g + 1) // 2

        def sums(i):
            if i not in sum_tiles:
                sum_columns = work.tile([P, 4], F32, bufs=5)
                sum_tiles[i] = sum_columns
            return sum_tiles[i]

        def y_sum(g):
            column = 1 if g % 2 == 1 else 2
            return sums(pair(g))[:, column : column + 1]

        def square_sum(g):
            column = 0 if g % 2 == 1 else 3
            return sums(pair(g) + 1)[:, column : column + 1]

        def product(g):
            y = resident.tile([P, J * QD], F32, name="y", bufs=GROUPS)
            nc.vector.scalar_tensor_tensor(
                out=y[:],
                in0=biased_tiles[g][:].rearrange("p j q -> p (j q)"),
                scalar=1.0,
                in1=g_tiles[g][:].rearrange("p j q -> p (j q)"),
                op0=ALU.mult,
                op1=ALU.mult,
                accum_out=y_sum(g),
            )
            y_tiles[g] = y

        def statistics(i):
            stats = psum.tile([P, 4], F32, tag="stats", bufs=1)
            columns = slice({0: 2, 1: 1}.get(i, 0), 3 if i == 0 else 4)
            nc.tensor.matmul(
                out=stats[:, columns], lhsT=neg_sample_mean[:], rhs=sums(i)[:, columns], start=True, stop=True
            )
            neg_mean_psums[i] = stats
            neg_variance_psums[i - 1] = stats

        def pair_means(i):
            neg_mean = work.tile([P, 2], F32, bufs=4)
            lo = 1 if i == 0 else 0
            nc.scalar.copy(out=neg_mean[:, lo:2], in_=neg_mean_psums[i][:, 1 + lo : 3])
            neg_means[2 * i - 1] = neg_mean[:, 0:1]
            neg_means[2 * i] = neg_mean[:, 1:2]

        def inverse_deviation(out, neg_variance):
            nc.scalar.activation(
                out=out, in_=neg_variance, func=ACT.Abs_reciprocal_sqrt, bias=eps[:], scale=-1.0
            )

        def pair_deviations(i):
            rstd = work.tile([P, 2], F32, bufs=4)
            lo = 1 if i == 0 else 0
            inverse_deviation(rstd[:, lo:2], neg_variance_psums[i][:, 3 * lo : 4 : 3])
            rstds[2 * i - 1] = rstd[:, 0:1]
            rstds[2 * i] = rstd[:, 1:2]

        def mean(g):
            neg_mean_ps = psum.tile([P, 1], F32, tag="flipped", bufs=4)
            nc.tensor.matmul(out=neg_mean_ps[:], lhsT=neg_sample_mean[:], rhs=y_sum(g), start=True, stop=True)
            neg_mean_psums[g, 1] = neg_mean_ps

        def copy_mean(g):
            neg_mean_of_one = work.tile([P, 1], F32, bufs=4)
            nc.scalar.copy(out=neg_mean_of_one[:], in_=neg_mean_psums[g, 1][:])
            neg_means[g] = neg_mean_of_one[:]

        def variance(g):
            neg_variance_ps = psum.tile([P, 1], F32, tag="flipped", bufs=4)
            nc.tensor.matmul(
                out=neg_variance_ps[:], lhsT=neg_sample_mean[:], rhs=square_sum(g), start=True, stop=True
            )
            neg_variance_psums[g, 1] = neg_variance_ps

        def deviation(g):
            rstd_of_one = work.tile([P, 1], F32, bufs=4)
            inverse_deviation(rstd_of_one[:], neg_variance_psums[g, 1][:])
            rstds[g] = rstd_of_one[:]

        def squares(g):
            squared = work.tile([P, J * QD], BF16, bufs=2)
            nc.scalar.activation(
                out=squared[:],
                in_=y_tiles[g][:],
                func=ACT.Square,
                bias=neg_means[g],
                scale=1.0,
                accum_out=square_sum(g),
            )

        def finish(g):
            y = y_tiles[g]
            engine = nc.vector if g >= LAST - 2 else nc.gpsimd
            engine.tensor_scalar(
                out=y[:], in0=y[:], scalar1=neg_means[g], scalar2=rstds[g], op0=ALU.add, op1=ALU.mult
            )
            nc.sync.dma_start(out=out_groups[g], in_=y[:])

        def run(stage, g, *args):
            if 0 <= g < GROUPS:
                stage(g, *args)

        first_half, second_half = range(0, J // 2), range(J // 2, J)
        with tc.manual_schedule():
            flip_x(0, first_half)
            prepare_weights()
            flip_x(0, second_half)
            quantise(0, first_half)
            quantise(0, second_half)
            flip_x(1)
            multiply_q(0)
            flip_kv(0)
            copy_kv(0)
            flip_x(2, first_half)
            multiply_g(0)
            flip_kv(1)
            flip_x(2, second_half)
            quantise(1)
            add_bias(0)
            copy_kv(1)
            product(0)
            multiply_q(1)
            flip_kv(2)
            for k in range(1, LAST):
                if k > 1:
                    add_bias(k - 1)
                copy_kv(k + 1)
                if k > 1:
                    product(k - 1)
                if k + 1 == LAST:
                    quantise(LAST, first_half)
                    quantise(LAST, second_half)
                else:
                    quantise(k + 1)
                if k % 2 == 1:
                    run(squares, k - 3)
                run(flip_x, k + 2, first_half)
                if k % 2 == 0:
                    pair_means(k // 2 - 1)
                    if k >= 4:
                        pair_deviations(k // 2 - 2)
                        run(finish, k - 5)
                        finish(k - 4)
                run(flip_x, k + 2, second_half)
                if k % 2 == 0:
                    run(squares, k - 3)
                run(flip_kv, k + 2)
                if k > 1:
                    multiply_q(k)
                multiply_g(k)
                if k % 2 == 1:
                    statistics((k - 1) // 2)
            mean(LAST - 2)
            squares(LAST - 3)
            copy_mean(LAST - 2)
            multiply_q(LAST, first_half)
            multiply_q(LAST, second_half)
            multiply_g(LAST)
            add_bias(LAST - 1)
            add_bias(LAST, first_half)
            product(LAST - 1)
            add_bias(LAST, second_half)
            variance(LAST - 4)
            variance(LAST - 3)
            mean(LAST - 1)
            squares(LAST - 2)
            deviation(LAST - 4)
            finish(LAST - 4)
            deviation(LAST - 3)
            finish(LAST - 3)
            copy_mean(LAST - 1)
            product(LAST)
            variance(LAST - 2)
            mean(LAST)
            squares(LAST - 1)
            copy_mean(LAST)
            deviation(LAST - 2)
            finish(LAST - 2)
            squares(LAST)
            variance(LAST - 1)
            deviation(LAST - 1)
            finish(LAST - 1)
            variance(LAST)
            deviation(LAST)
            finish(LAST)
